import numpy as np
import ml_dtypes


def mxq(x, axis, fmt="e4m3"):
    dtype, down = {"e4m3": (ml_dtypes.float8_e4m3fn, 7), "e5m2": (ml_dtypes.float8_e5m2, 14)}[fmt]
    v = np.moveaxis(np.asarray(x, np.float32).astype(ml_dtypes.bfloat16).astype(np.float64), axis, -1)
    blocks = v.reshape(v.shape[:-1] + (-1, 32))
    amax = np.abs(blocks).max(-1, keepdims=True)
    byte = np.maximum(np.where(amax > 0, np.frexp(amax)[1] - 1 + 127, 0) - down, 1)
    scale = np.exp2(byte - 127.0)
    codes = (blocks / scale).astype(np.float32).astype(dtype).astype(np.float64)
    return np.moveaxis((codes * scale).reshape(v.shape), -1, axis)


WIDE = False


def mx_kscale(k):
    if not WIDE:
        return np.ones(k)
    levels = np.array([10, -10, 5, -5, 0])
    a = np.random.permutation(np.resize(levels, k // 512 * 4)).reshape(k // 512, 4)
    idx = np.arange(k)
    return np.exp2(a[idx // 512, idx % 128 // 32])


BF16 = ml_dtypes.bfloat16


def bf(x):
    return np.asarray(x, np.float32).astype(BF16)


def f64(x):
    return np.asarray(x).astype(np.float64)


E2M1 = np.array([0.0, 0.5, 1.0, 1.5, 2.0, 3.0, 4.0, 6.0, -0.0, -0.5, -1.0, -1.5, -2.0, -3.0, -4.0, -6.0])


def pack_weight(w, fmt):
    k, n = w.shape
    w = f64(bf(w)).reshape(k // 32, 32, n)
    amax = np.abs(w).max(1)
    if fmt == "e4m3":
        byte = np.frexp(amax)[1] - 1 + 127 - 7
    else:
        mant, ex = np.frexp(amax / 6.0)
        byte = np.where(mant > 0.5, ex, ex - 1) + 127
    byte = np.clip(np.where(amax > 0, byte, 1), 1, 254)
    scaled = (w * np.exp2(127.0 - byte)[:, None, :]).reshape(k, n).astype(np.float32)
    by_word = np.ascontiguousarray(scaled.reshape(k // 512, 128, 4, n).transpose(0, 1, 3, 2))
    if fmt == "e4m3":
        words = by_word.astype(ml_dtypes.float8_e4m3fn).view(np.uint8)
    else:
        c = by_word.astype(ml_dtypes.float4_e2m1fn).view(np.uint8) & 0xF
        words = c[..., 0::2] | (c[..., 1::2] << 4)
    return np.ascontiguousarray(words), np.ascontiguousarray(byte.astype(np.uint8).reshape(k // 512, 16, n))


def unpack_weight(words, scales, fmt):
    g, p, n, _ = words.shape
    if fmt == "e4m3":
        vals = np.ascontiguousarray(words).view(ml_dtypes.float8_e4m3fn).astype(np.float64)
    else:
        nib = np.empty((g, p, n, 4), np.uint8)
        nib[..., 0::2] = words & 0xF
        nib[..., 1::2] = words >> 4
        vals = E2M1[nib]
    vals = vals * np.repeat(np.exp2(scales.astype(np.float64) - 127.0), 8, axis=1)[..., None]
    return vals.transpose(0, 1, 3, 2).reshape(g * 512, n)


C, F, H, B, S = 2, 128, 512, 16, 256
FMT = "e4m3"


def pack_stack(stack):
    st = np.swapaxes(stack, 1, 2)
    cat = st.reshape(-1, st.shape[-1])
    return pack_weight(cat, FMT)


def setup_inputs():
    s, t = mx_kscale(H), mx_kscale(H)
    g = 0.3 / np.sqrt(H)
    hidden = bf(np.random.standard_normal((B, S, H)) * s)
    emb_words, emb_scales = pack_stack(np.random.standard_normal((C, F, H)) * 0.3 * t)
    Wk_words, Wk_scales = pack_stack(np.random.standard_normal((C, H, H)) * g / t[:, None] / s)
    Wq_words, Wq_scales = pack_stack(np.random.standard_normal((C, H, H)) * g * t[:, None] / s)
    vsum = bf(np.random.standard_normal((C, B, S)))
    return {"hidden": hidden,
            "emb_words": emb_words, "emb_scales": emb_scales,
            "Wk_words": Wk_words, "Wk_scales": Wk_scales,
            "Wq_words": Wq_words, "Wq_scales": Wq_scales,
            "vsum": vsum}


def reference(hidden, emb_words, emb_scales, Wk_words, Wk_scales, Wq_words, Wq_scales, vsum):
    hq = mxq(f64(hidden), 2, "e4m3")[None]
    key = hq @ unpack_weight(Wk_words, Wk_scales, FMT).reshape(C, H, H)[:, None]
    query = hq @ unpack_weight(Wq_words, Wq_scales, FMT).reshape(C, H, H)[:, None]
    kt = mxq(key, 3, "e4m3").transpose(0, 1, 3, 2)
    att_tok = mxq(query, 3, "e4m3") @ kt
    att_lab = unpack_weight(emb_words, emb_scales, FMT).reshape(C, H, F).swapaxes(1, 2)[:, None] @ kt
    attention = np.concatenate([att_tok, att_lab], axis=2).transpose(1, 0, 2, 3)
    return attention * f64(vsum).transpose(1, 0, 2)[:, :, None, :]

@@ -1,0 +1,198 @@
+from contextlib import ExitStack
+
+import concourse.mybir as mybir
+from concourse.masks import make_identity
+
+F32 = mybir.dt.float32
+BF16 = mybir.dt.bfloat16
+U8 = mybir.dt.uint8
+U32 = mybir.dt.uint32
+I32 = mybir.dt.int32
+FP8X4 = mybir.dt.float8_e4m3fn_x4
+
+P = 128
+PACK = 4
+B, C, S, H, F = 16, 2, 256, 512, 128
+TOKEN_TILES = S // P
+PAIRS = 2
+BANK = 512
+Q, K = 0, 1
+ROW_TILES = (S + F) // P
+
+STEP_PROJECT = 1
+STEP_TURN = 3
+STEP_SCORE = 4
+
+FLOPS = 2 * B * S * H * H * C * 2 + 2 * B * C * (S + F) * S * H
+
+
+def load_packed_weight(nc, codes, planes, words, scales):
+    for quadrant in range(4):
+        rows = slice(4 * quadrant, 4 * quadrant + 4)
+        nc.sync.dma_start(
+            out=planes[32 * quadrant : 32 * quadrant + 4].bitcast(I32),
+            in_=scales[:, rows, :].rearrange("g r n -> r g n").bitcast(I32),
+        )
+    nc.sync.dma_start(out=codes.bitcast(I32), in_=words.rearrange("g p n t -> p g (n t)").bitcast(I32))
+
+
+def tile_relationtagger_pa_t_e_kernel(
+    tc, hidden, emb_words, emb_scales, Wk_words, Wk_scales, Wq_words, Wq_scales, vsum, out
+):
+    nc = tc.nc
+    with ExitStack() as ctx:
+        ctx.enter_context(tc.manual_schedule())
+        keep = ctx.enter_context(tc.tile_pool(name="keep", bufs=1))
+        h_stage = ctx.enter_context(tc.tile_pool(name="h_stage", bufs=2))
+        h_quant = ctx.enter_context(tc.tile_pool(name="h_quant", bufs=3))
+        rows_pool = ctx.enter_context(tc.tile_pool(name="rows", bufs=2 * C * (STEP_TURN - STEP_PROJECT + 1)))
+        qk_stage = ctx.enter_context(tc.tile_pool(name="qk_stage", bufs=2))
+        qk_quant = ctx.enter_context(tc.tile_pool(name="qk_quant", bufs=3))
+        out_pool = ctx.enter_context(tc.tile_pool(name="out", bufs=3))
+        psum = ctx.enter_context(tc.psum_pool(name="psum", bufs=8))
+
+        hid = keep.tile([P, B, TOKEN_TILES, H], BF16, name="hid")
+        w_codes = keep.tile([P, 2, C, H], U32, name="w_codes", align_bytes=64)
+        w_planes = keep.tile([P, 2, C, H], U8, name="w_planes", align_bytes=64)
+        emb_codes = keep.tile([P, C, F], U32, name="emb_codes", align_bytes=64)
+        emb_planes = keep.tile([P, C, F], U8, name="emb_planes", align_bytes=64)
+        gate = keep.tile([P, C, B, S], BF16, name="gate")
+        ident = keep.tile([P, P], F32, name="ident")
+
+        nc.vector.memset(w_planes[:].bitcast(I32), 0)
+        nc.vector.memset(emb_planes[:].bitcast(I32), 0)
+        make_identity(nc, ident[:])
+
+        def load_hidden(b):
+            nc.sync.dma_start(out=hid[:, b], in_=hidden[b].rearrange("(s p) h -> p s h", p=P))
+
+        load_hidden(0)
+        load_packed_weight(nc, w_codes[:, Q], w_planes[:, Q], Wq_words, Wq_scales)
+        load_packed_weight(nc, w_codes[:, K], w_planes[:, K], Wk_words, Wk_scales)
+        load_hidden(1)
+        load_packed_weight(nc, emb_codes[:], emb_planes[:], emb_words, emb_scales)
+        load_hidden(2)
+        nc.sync.dma_start(
+            out=gate[:].rearrange("p c b j -> p (c b j)"),
+            in_=vsum.rearrange("c b j -> (c b j)").partition_broadcast(P),
+        )
+        for b in range(3, B):
+            load_hidden(b)
+
+        def turn(word_rows, grouped, copy):
+            bank = psum.tile([P, BANK], F32, name="bank", tag="bank")
+            for s in range(TOKEN_TILES):
+                for u in range(PAIRS):
+                    col = (s * PAIRS + u) * P
+                    nc.tensor.transpose(bank[:, col : col + P], word_rows(s, u), ident[:])
+            copy(
+                out=grouped.bitcast(F32).rearrange("p (s j u) -> p s j u", s=TOKEN_TILES, u=PAIRS),
+                in_=bank[:].rearrange("p (s u j) -> p s j u", s=TOKEN_TILES, u=PAIRS),
+            )
+
+        h_grouped, h_codes, h_planes = {}, {}, {}
+        rows, qk_codes, qk_planes = {}, {}, {}
+
+        def turn_hidden(b):
+            h_grouped[b] = h_stage.tile([P, PACK * S], BF16, name="h_grouped", align_bytes=64)
+            turn(
+                lambda s, u: hid[:, b, s, :].bitcast(F32)[:, u : H // 2 : PAIRS],
+                h_grouped[b][:],
+                nc.scalar.copy,
+            )
+
+        def quantise_hidden(b):
+            h_codes[b] = h_quant.tile([P, S], U32, name="h_codes", align_bytes=64)
+            h_planes[b] = h_quant.tile([P, S], U8, name="h_planes", align_bytes=64)
+            nc.vector.quantize_mx(out=h_codes[b][:].bitcast(FP8X4), scales=h_planes[b][:], in_=h_grouped[b][:])
+
+        def project(b):
+            for c in range(C):
+                for kind in (Q, K):
+                    rows[b, c, kind] = rows_pool.tile([P, TOKEN_TILES, H], BF16, name="rows")
+                    for s in range(TOKEN_TILES):
+                        tokens = slice(s * P, (s + 1) * P)
+                        bank = psum.tile([P, BANK], F32, name="bank", tag="bank")
+                        nc.tensor.matmul_mx(
+                            out=bank[:],
+                            lhsT=h_codes[b][:, tokens].bitcast(FP8X4),
+                            lhsT_scale=h_planes[b][:, tokens],
+                            rhs=w_codes[:, kind, c, :].bitcast(FP8X4),
+                            rhs_scale=w_planes[:, kind, c, :],
+                            start=True,
+                            stop=True,
+                        )
+                        nc.scalar.copy(
+                            out=rows[b, c, kind][:, s, :].rearrange("t (u p e) -> t u p e", u=PAIRS, e=2),
+                            in_=bank[:].rearrange("t (p u e) -> t u p e", u=PAIRS, e=2),
+                        )
+
+        def turn_and_quantise(b):
+            grouped = qk_stage.tile([P, C, 2, PACK * S], BF16, name="grouped", align_bytes=64)
+            qk_codes[b] = qk_quant.tile([P, C, 2, S], U32, name="qk_codes", align_bytes=64)
+            qk_planes[b] = qk_quant.tile([P, C, 2, S], U8, name="qk_planes", align_bytes=64)
+            for c in range(C):
+                for kind in (Q, K):
+                    src = rows[b, c, kind]
+                    turn(
+                        lambda s, u: src[:, s, :].bitcast(F32)[:, u * P : (u + 1) * P],
+                        grouped[:, c, kind, :],
+                        nc.vector.tensor_copy,
+                    )
+                nc.vector.quantize_mx(
+                    out=qk_codes[b][:, c].rearrange("p k j -> p (k j)").bitcast(FP8X4),
+                    scales=qk_planes[b][:, c].rearrange("p k j -> p (k j)"),
+                    in_=grouped[:, c].rearrange("p k x -> p (k x)"),
+                )
+
+        def score_pass(dst, b, c, lhsT, lhsT_scale):
+            nc.tensor.matmul_mx(
+                out=dst,
+                lhsT=lhsT.bitcast(FP8X4),
+                lhsT_scale=lhsT_scale,
+                rhs=qk_codes[b][:, c, K, :].bitcast(FP8X4),
+                rhs_scale=qk_planes[b][:, c, K, :],
+                start=True,
+                stop=True,
+            )
+
+        def score(b):
+            result = out_pool.tile([P, C, ROW_TILES, S], F32, name="result")
+            for c in range(C):
+                bank = psum.tile([P, BANK], F32, name="bank", tag="bank")
+                for s in range(TOKEN_TILES):
+                    tokens = slice(s * P, (s + 1) * P)
+                    score_pass(
+                        bank[:, s * S : (s + 1) * S], b, c, qk_codes[b][:, c, Q, tokens], qk_planes[b][:, c, Q, tokens]
+                    )
+                nc.vector.tensor_tensor(
+                    out=result[:, c, 0:TOKEN_TILES, :],
+                    in0=bank[:].rearrange("p (s j) -> p s j", s=TOKEN_TILES),
+                    in1=gate[:, c, b, :].unsqueeze(1).to_broadcast([P, TOKEN_TILES, S]),
+                    op=mybir.AluOpType.mult,
+                )
+            bank = psum.tile([P, BANK], F32, name="bank", tag="bank")
+            for c in range(C):
+                score_pass(bank[:, c * S : (c + 1) * S], b, c, emb_codes[:, c, :], emb_planes[:, c, :])
+            nc.vector.tensor_tensor(
+                out=result[:, :, TOKEN_TILES, :],
+                in0=bank[:].rearrange("p (c j) -> p c j", c=C),
+                in1=gate[:, :, b, :],
+                op=mybir.AluOpType.mult,
+            )
+            nc.sync.dma_start(
+                out=out[b].rearrange("c (s p) j -> p (c s) j", p=P),
+                in_=result[:].rearrange("p c s j -> p (c s) j"),
+            )
+
+        for step in range(B + STEP_SCORE):
+            if step < B:
+                turn_hidden(step)
+            if 0 <= step - STEP_TURN < B:
+                turn_and_quantise(step - STEP_TURN)
+            if step < B:
+                quantise_hidden(step)
+            if 0 <= step - STEP_PROJECT < B:
+                project(step - STEP_PROJECT)
+            if 0 <= step - STEP_SCORE < B:
+                score(step - STEP_SCORE)

@@ -20,8 +20,11 @@ Q, K = 0, 1
 ROW_TILES = (S + F) // P
 
 STEP_PROJECT = 1
-STEP_TURN = 3
-STEP_SCORE = 4
+STEP_TURN = (2, 3)
+STEP_SCORE = 3
+
+SCALAR_BANKS = 5
+VECTOR_BANKS = 3
 
 FLOPS = 2 * B * S * H * H * C * 2 + 2 * B * C * (S + F) * S * H
 
@@ -45,11 +48,12 @@ def tile_relationtagger_pa_t_e_kernel(
         keep = ctx.enter_context(tc.tile_pool(name="keep", bufs=1))
         h_stage = ctx.enter_context(tc.tile_pool(name="h_stage", bufs=2))
         h_quant = ctx.enter_context(tc.tile_pool(name="h_quant", bufs=3))
-        rows_pool = ctx.enter_context(tc.tile_pool(name="rows", bufs=2 * C * (STEP_TURN - STEP_PROJECT + 1)))
-        qk_stage = ctx.enter_context(tc.tile_pool(name="qk_stage", bufs=2))
-        qk_quant = ctx.enter_context(tc.tile_pool(name="qk_quant", bufs=3))
+        rows_pool = ctx.enter_context(tc.tile_pool(name="rows", bufs=12))
+        qk_stage = ctx.enter_context(tc.tile_pool(name="qk_stage", bufs=3))
+        qk_quant = ctx.enter_context(tc.tile_pool(name="qk_quant", bufs=5))
         out_pool = ctx.enter_context(tc.tile_pool(name="out", bufs=3))
-        psum = ctx.enter_context(tc.psum_pool(name="psum", bufs=8))
+        psum_scalar = ctx.enter_context(tc.psum_pool(name="psum_scalar", bufs=SCALAR_BANKS))
+        psum_vector = ctx.enter_context(tc.psum_pool(name="psum_vector", bufs=VECTOR_BANKS))
 
         hid = keep.tile([P, B, TOKEN_TILES, H], BF16, name="hid")
         w_codes = keep.tile([P, 2, C, H], U32, name="w_codes", align_bytes=64)
@@ -79,7 +83,7 @@ def tile_relationtagger_pa_t_e_kernel(
         for b in range(3, B):
             load_hidden(b)
 
-        def turn(word_rows, grouped, copy):
+        def turn(word_rows, grouped, psum, copy):
             bank = psum.tile([P, BANK], F32, name="bank", tag="bank")
             for s in range(TOKEN_TILES):
                 for u in range(PAIRS):
@@ -98,6 +102,7 @@ def tile_relationtagger_pa_t_e_kernel(
             turn(
                 lambda s, u: hid[:, b, s, :].bitcast(F32)[:, u : H // 2 : PAIRS],
                 h_grouped[b][:],
+                psum_scalar,
                 nc.scalar.copy,
             )
 
@@ -106,52 +111,51 @@ def tile_relationtagger_pa_t_e_kernel(
             h_planes[b] = h_quant.tile([P, S], U8, name="h_planes", align_bytes=64)
             nc.vector.quantize_mx(out=h_codes[b][:].bitcast(FP8X4), scales=h_planes[b][:], in_=h_grouped[b][:])
 
-        def project(b):
-            for c in range(C):
-                for kind in (Q, K):
-                    rows[b, c, kind] = rows_pool.tile([P, TOKEN_TILES, H], BF16, name="rows")
-                    for s in range(TOKEN_TILES):
-                        tokens = slice(s * P, (s + 1) * P)
-                        bank = psum.tile([P, BANK], F32, name="bank", tag="bank")
-                        nc.tensor.matmul_mx(
-                            out=bank[:],
-                            lhsT=h_codes[b][:, tokens].bitcast(FP8X4),
-                            lhsT_scale=h_planes[b][:, tokens],
-                            rhs=w_codes[:, kind, c, :].bitcast(FP8X4),
-                            rhs_scale=w_planes[:, kind, c, :],
-                            start=True,
-                            stop=True,
-                        )
-                        nc.scalar.copy(
-                            out=rows[b, c, kind][:, s, :].rearrange("t (u p e) -> t u p e", u=PAIRS, e=2),
-                            in_=bank[:].rearrange("t (p u e) -> t u p e", u=PAIRS, e=2),
-                        )
-
-        def turn_and_quantise(b):
-            grouped = qk_stage.tile([P, C, 2, PACK * S], BF16, name="grouped", align_bytes=64)
-            qk_codes[b] = qk_quant.tile([P, C, 2, S], U32, name="qk_codes", align_bytes=64)
-            qk_planes[b] = qk_quant.tile([P, C, 2, S], U8, name="qk_planes", align_bytes=64)
-            for c in range(C):
-                for kind in (Q, K):
-                    src = rows[b, c, kind]
-                    turn(
-                        lambda s, u: src[:, s, :].bitcast(F32)[:, u * P : (u + 1) * P],
-                        grouped[:, c, kind, :],
-                        nc.vector.tensor_copy,
+        def project(b, c):
+            for kind in (Q, K):
+                rows[b, c, kind] = rows_pool.tile([P, TOKEN_TILES, H], BF16, name="rows")
+                for s in range(TOKEN_TILES):
+                    tokens = slice(s * P, (s + 1) * P)
+                    bank = psum_scalar.tile([P, BANK], F32, name="bank", tag="bank")
+                    nc.tensor.matmul_mx(
+                        out=bank[:],
+                        lhsT=h_codes[b][:, tokens].bitcast(FP8X4),
+                        lhsT_scale=h_planes[b][:, tokens],
+                        rhs=w_codes[:, kind, c, :].bitcast(FP8X4),
+                        rhs_scale=w_planes[:, kind, c, :],
+                        start=True,
+                        stop=True,
                     )
-                nc.vector.quantize_mx(
-                    out=qk_codes[b][:, c].rearrange("p k j -> p (k j)").bitcast(FP8X4),
-                    scales=qk_planes[b][:, c].rearrange("p k j -> p (k j)"),
-                    in_=grouped[:, c].rearrange("p k x -> p (k x)"),
+                    nc.scalar.copy(
+                        out=rows[b, c, kind][:, s, :].rearrange("t (u p e) -> t u p e", u=PAIRS, e=2),
+                        in_=bank[:].rearrange("t (p u e) -> t u p e", u=PAIRS, e=2),
+                    )
+
+        def turn_and_quantise(b, c):
+            grouped = qk_stage.tile([P, 2, PACK * S], BF16, name="grouped", align_bytes=64)
+            qk_codes[b, c] = qk_quant.tile([P, 2, S], U32, name="qk_codes", align_bytes=64)
+            qk_planes[b, c] = qk_quant.tile([P, 2, S], U8, name="qk_planes", align_bytes=64)
+            for kind in (Q, K):
+                src = rows[b, c, kind]
+                turn(
+                    lambda s, u: src[:, s, :].bitcast(F32)[:, u * P : (u + 1) * P],
+                    grouped[:, kind, :],
+                    psum_vector,
+                    nc.vector.tensor_copy,
                 )
+            nc.vector.quantize_mx(
+                out=qk_codes[b, c][:].rearrange("p k j -> p (k j)").bitcast(FP8X4),
+                scales=qk_planes[b, c][:].rearrange("p k j -> p (k j)"),
+                in_=grouped[:].rearrange("p k x -> p (k x)"),
+            )
 
         def score_pass(dst, b, c, lhsT, lhsT_scale):
             nc.tensor.matmul_mx(
                 out=dst,
                 lhsT=lhsT.bitcast(FP8X4),
                 lhsT_scale=lhsT_scale,
-                rhs=qk_codes[b][:, c, K, :].bitcast(FP8X4),
-                rhs_scale=qk_planes[b][:, c, K, :],
+                rhs=qk_codes[b, c][:, K, :].bitcast(FP8X4),
+                rhs_scale=qk_planes[b, c][:, K, :],
                 start=True,
                 stop=True,
             )
@@ -159,11 +163,11 @@ def tile_relationtagger_pa_t_e_kernel(
         def score(b):
             result = out_pool.tile([P, C, ROW_TILES, S], F32, name="result")
             for c in range(C):
-                bank = psum.tile([P, BANK], F32, name="bank", tag="bank")
+                bank = psum_vector.tile([P, BANK], F32, name="bank", tag="bank")
                 for s in range(TOKEN_TILES):
                     tokens = slice(s * P, (s + 1) * P)
                     score_pass(
-                        bank[:, s * S : (s + 1) * S], b, c, qk_codes[b][:, c, Q, tokens], qk_planes[b][:, c, Q, tokens]
+                        bank[:, s * S : (s + 1) * S], b, c, qk_codes[b, c][:, Q, tokens], qk_planes[b, c][:, Q, tokens]
                     )
                 nc.vector.tensor_tensor(
                     out=result[:, c, 0:TOKEN_TILES, :],
@@ -171,7 +175,7 @@ def tile_relationtagger_pa_t_e_kernel(
                     in1=gate[:, c, b, :].unsqueeze(1).to_broadcast([P, TOKEN_TILES, S]),
                     op=mybir.AluOpType.mult,
                 )
-            bank = psum.tile([P, BANK], F32, name="bank", tag="bank")
+            bank = psum_vector.tile([P, BANK], F32, name="bank", tag="bank")
             for c in range(C):
                 score_pass(bank[:, c * S : (c + 1) * S], b, c, emb_codes[:, c, :], emb_planes[:, c, :])
             nc.vector.tensor_tensor(
@@ -185,14 +189,17 @@ def tile_relationtagger_pa_t_e_kernel(
                 in_=result[:].rearrange("p c s j -> p (c s) j"),
             )
 
-        for step in range(B + STEP_SCORE):
+        for step in range(B + STEP_SCORE + 1):
             if step < B:
                 turn_hidden(step)
-            if 0 <= step - STEP_TURN < B:
-                turn_and_quantise(step - STEP_TURN)
+            for c in reversed(range(C)):
+                if 0 <= step - STEP_TURN[c] < B:
+                    turn_and_quantise(step - STEP_TURN[c], c)
             if step < B:
                 quantise_hidden(step)
             if 0 <= step - STEP_PROJECT < B:
-                project(step - STEP_PROJECT)
+                project(step - STEP_PROJECT, 0)
             if 0 <= step - STEP_SCORE < B:
                 score(step - STEP_SCORE)
+            if 0 <= step - STEP_PROJECT < B:
+                project(step - STEP_PROJECT, 1)

@@ -16,15 +16,16 @@ B, C, S, H, F = 16, 2, 256, 512, 128
 TOKEN_TILES = S // P
 PAIRS = 2
 BANK = 512
+PSUM_BANKS = 8
 Q, K = 0, 1
 ROW_TILES = (S + F) // P
 
 STEP_PROJECT = 1
-STEP_TURN = (2, 3)
-STEP_SCORE = 3
+STEP_TURN = 3
+STEP_SCORE = 4
 
-SCALAR_BANKS = 5
-VECTOR_BANKS = 3
+FILLING = 2
+DRAINING = 2
 
 FLOPS = 2 * B * S * H * H * C * 2 + 2 * B * C * (S + F) * S * H
 
@@ -48,12 +49,11 @@ def tile_relationtagger_pa_t_e_kernel(
         keep = ctx.enter_context(tc.tile_pool(name="keep", bufs=1))
         h_stage = ctx.enter_context(tc.tile_pool(name="h_stage", bufs=2))
         h_quant = ctx.enter_context(tc.tile_pool(name="h_quant", bufs=3))
-        rows_pool = ctx.enter_context(tc.tile_pool(name="rows", bufs=12))
-        qk_stage = ctx.enter_context(tc.tile_pool(name="qk_stage", bufs=3))
-        qk_quant = ctx.enter_context(tc.tile_pool(name="qk_quant", bufs=5))
+        rows_pool = ctx.enter_context(tc.tile_pool(name="rows", bufs=2 * C * (STEP_TURN - STEP_PROJECT + 1)))
+        qk_stage = ctx.enter_context(tc.tile_pool(name="qk_stage", bufs=2))
+        qk_quant = ctx.enter_context(tc.tile_pool(name="qk_quant", bufs=3))
         out_pool = ctx.enter_context(tc.tile_pool(name="out", bufs=3))
-        psum_scalar = ctx.enter_context(tc.psum_pool(name="psum_scalar", bufs=SCALAR_BANKS))
-        psum_vector = ctx.enter_context(tc.psum_pool(name="psum_vector", bufs=VECTOR_BANKS))
+        psum = ctx.enter_context(tc.psum_pool(name="psum", bufs=PSUM_BANKS))
 
         hid = keep.tile([P, B, TOKEN_TILES, H], BF16, name="hid")
         w_codes = keep.tile([P, 2, C, H], U32, name="w_codes", align_bytes=64)
@@ -73,17 +73,17 @@ def tile_relationtagger_pa_t_e_kernel(
         load_hidden(0)
         load_packed_weight(nc, w_codes[:, Q], w_planes[:, Q], Wq_words, Wq_scales)
         load_packed_weight(nc, w_codes[:, K], w_planes[:, K], Wk_words, Wk_scales)
-        load_hidden(1)
+        for b in range(1, STEP_SCORE):
+            load_hidden(b)
         load_packed_weight(nc, emb_codes[:], emb_planes[:], emb_words, emb_scales)
-        load_hidden(2)
         nc.sync.dma_start(
             out=gate[:].rearrange("p c b j -> p (c b j)"),
             in_=vsum.rearrange("c b j -> (c b j)").partition_broadcast(P),
         )
-        for b in range(3, B):
+        for b in range(STEP_SCORE, B):
             load_hidden(b)
 
-        def turn(word_rows, grouped, psum, copy):
+        def transpose_words(word_rows, grouped, copy):
             bank = psum.tile([P, BANK], F32, name="bank", tag="bank")
             for s in range(TOKEN_TILES):
                 for u in range(PAIRS):
@@ -95,14 +95,13 @@ def tile_relationtagger_pa_t_e_kernel(
             )
 
         h_grouped, h_codes, h_planes = {}, {}, {}
-        rows, qk_codes, qk_planes = {}, {}, {}
+        rows, qk_grouped, qk_codes, qk_planes = {}, {}, {}, {}
 
-        def turn_hidden(b):
+        def transpose_hidden(b):
             h_grouped[b] = h_stage.tile([P, PACK * S], BF16, name="h_grouped", align_bytes=64)
-            turn(
+            transpose_words(
                 lambda s, u: hid[:, b, s, :].bitcast(F32)[:, u : H // 2 : PAIRS],
                 h_grouped[b][:],
-                psum_scalar,
                 nc.scalar.copy,
             )
 
@@ -116,7 +115,7 @@ def tile_relationtagger_pa_t_e_kernel(
                 rows[b, c, kind] = rows_pool.tile([P, TOKEN_TILES, H], BF16, name="rows")
                 for s in range(TOKEN_TILES):
                     tokens = slice(s * P, (s + 1) * P)
-                    bank = psum_scalar.tile([P, BANK], F32, name="bank", tag="bank")
+                    bank = psum.tile([P, BANK], F32, name="bank", tag="bank")
                     nc.tensor.matmul_mx(
                         out=bank[:],
                         lhsT=h_codes[b][:, tokens].bitcast(FP8X4),
@@ -126,36 +125,41 @@ def tile_relationtagger_pa_t_e_kernel(
                         start=True,
                         stop=True,
                     )
-                    nc.scalar.copy(
+                    copy = nc.vector.tensor_copy if b < FILLING and s == 1 else nc.scalar.copy
+                    copy(
                         out=rows[b, c, kind][:, s, :].rearrange("t (u p e) -> t u p e", u=PAIRS, e=2),
                         in_=bank[:].rearrange("t (p u e) -> t u p e", u=PAIRS, e=2),
                     )
 
-        def turn_and_quantise(b, c):
-            grouped = qk_stage.tile([P, 2, PACK * S], BF16, name="grouped", align_bytes=64)
-            qk_codes[b, c] = qk_quant.tile([P, 2, S], U32, name="qk_codes", align_bytes=64)
-            qk_planes[b, c] = qk_quant.tile([P, 2, S], U8, name="qk_planes", align_bytes=64)
-            for kind in (Q, K):
-                src = rows[b, c, kind]
-                turn(
-                    lambda s, u: src[:, s, :].bitcast(F32)[:, u * P : (u + 1) * P],
-                    grouped[:, kind, :],
-                    psum_vector,
-                    nc.vector.tensor_copy,
+        def transpose_projections(b):
+            qk_grouped[b] = qk_stage.tile([P, C, 2, PACK * S], BF16, name="qk_grouped", align_bytes=64)
+            for c in range(C):
+                for kind in (Q, K):
+                    src = rows[b, c, kind]
+                    on_scalar = b >= B - DRAINING or (c == 1 and kind == Q)
+                    transpose_words(
+                        lambda s, u: src[:, s, :].bitcast(F32)[:, u * P : (u + 1) * P],
+                        qk_grouped[b][:, c, kind, :],
+                        nc.scalar.copy if on_scalar else nc.vector.tensor_copy,
+                    )
+
+        def quantise_projections(b):
+            qk_codes[b] = qk_quant.tile([P, C, 2, S], U32, name="qk_codes", align_bytes=64)
+            qk_planes[b] = qk_quant.tile([P, C, 2, S], U8, name="qk_planes", align_bytes=64)
+            for c in range(C):
+                nc.vector.quantize_mx(
+                    out=qk_codes[b][:, c].rearrange("p k j -> p (k j)").bitcast(FP8X4),
+                    scales=qk_planes[b][:, c].rearrange("p k j -> p (k j)"),
+                    in_=qk_grouped[b][:, c].rearrange("p k x -> p (k x)"),
                 )
-            nc.vector.quantize_mx(
-                out=qk_codes[b, c][:].rearrange("p k j -> p (k j)").bitcast(FP8X4),
-                scales=qk_planes[b, c][:].rearrange("p k j -> p (k j)"),
-                in_=grouped[:].rearrange("p k x -> p (k x)"),
-            )
 
         def score_pass(dst, b, c, lhsT, lhsT_scale):
             nc.tensor.matmul_mx(
                 out=dst,
                 lhsT=lhsT.bitcast(FP8X4),
                 lhsT_scale=lhsT_scale,
-                rhs=qk_codes[b, c][:, K, :].bitcast(FP8X4),
-                rhs_scale=qk_planes[b, c][:, K, :],
+                rhs=qk_codes[b][:, c, K, :].bitcast(FP8X4),
+                rhs_scale=qk_planes[b][:, c, K, :],
                 start=True,
                 stop=True,
             )
@@ -163,11 +167,11 @@ def tile_relationtagger_pa_t_e_kernel(
         def score(b):
             result = out_pool.tile([P, C, ROW_TILES, S], F32, name="result")
             for c in range(C):
-                bank = psum_vector.tile([P, BANK], F32, name="bank", tag="bank")
+                bank = psum.tile([P, BANK], F32, name="bank", tag="bank")
                 for s in range(TOKEN_TILES):
                     tokens = slice(s * P, (s + 1) * P)
                     score_pass(
-                        bank[:, s * S : (s + 1) * S], b, c, qk_codes[b, c][:, Q, tokens], qk_planes[b, c][:, Q, tokens]
+                        bank[:, s * S : (s + 1) * S], b, c, qk_codes[b][:, c, Q, tokens], qk_planes[b][:, c, Q, tokens]
                     )
                 nc.vector.tensor_tensor(
                     out=result[:, c, 0:TOKEN_TILES, :],
@@ -175,7 +179,10 @@ def tile_relationtagger_pa_t_e_kernel(
                     in1=gate[:, c, b, :].unsqueeze(1).to_broadcast([P, TOKEN_TILES, S]),
                     op=mybir.AluOpType.mult,
                 )
-            bank = psum_vector.tile([P, BANK], F32, name="bank", tag="bank")
+                nc.sync.dma_start(
+                    out=out[b, c, 0:S, :].rearrange("(s p) j -> p s j", p=P), in_=result[:, c, 0:TOKEN_TILES, :]
+                )
+            bank = psum.tile([P, BANK], F32, name="bank", tag="bank")
             for c in range(C):
                 score_pass(bank[:, c * S : (c + 1) * S], b, c, emb_codes[:, c, :], emb_planes[:, c, :])
             nc.vector.tensor_tensor(
@@ -184,17 +191,14 @@ def tile_relationtagger_pa_t_e_kernel(
                 in1=gate[:, :, b, :],
                 op=mybir.AluOpType.mult,
             )
-            nc.sync.dma_start(
-                out=out[b].rearrange("c (s p) j -> p (c s) j", p=P),
-                in_=result[:].rearrange("p c s j -> p (c s) j"),
-            )
+            nc.sync.dma_start(out=out[b, :, S:, :].rearrange("c p j -> p c j"), in_=result[:, :, TOKEN_TILES, :])
 
-        for step in range(B + STEP_SCORE + 1):
+        for step in range(B + STEP_SCORE):
             if step < B:
-                turn_hidden(step)
-            for c in reversed(range(C)):
-                if 0 <= step - STEP_TURN[c] < B:
-                    turn_and_quantise(step - STEP_TURN[c], c)
+                transpose_hidden(step)
+            if 0 <= step - STEP_TURN < B:
+                transpose_projections(step - STEP_TURN)
+                quantise_projections(step - STEP_TURN)
             if step < B:
                 quantise_hidden(step)
             if 0 <= step - STEP_PROJECT < B:

@@ -24,8 +24,9 @@ STEP_PROJECT = 1
 STEP_TURN = 3
 STEP_SCORE = 4
 
+SCALAR_EVERY = 8
 FILLING = 2
-DRAINING = 2
+DRAINING = 1
 
 FLOPS = 2 * B * S * H * H * C * 2 + 2 * B * C * (S + F) * S * H
 
@@ -71,9 +72,10 @@ def tile_relationtagger_pa_t_e_kernel(
             nc.sync.dma_start(out=hid[:, b], in_=hidden[b].rearrange("(s p) h -> p s h", p=P))
 
         load_hidden(0)
+        load_hidden(1)
         load_packed_weight(nc, w_codes[:, Q], w_planes[:, Q], Wq_words, Wq_scales)
         load_packed_weight(nc, w_codes[:, K], w_planes[:, K], Wk_words, Wk_scales)
-        for b in range(1, STEP_SCORE):
+        for b in range(2, STEP_SCORE):
             load_hidden(b)
         load_packed_weight(nc, emb_codes[:], emb_planes[:], emb_words, emb_scales)
         nc.sync.dma_start(
@@ -136,7 +138,8 @@ def tile_relationtagger_pa_t_e_kernel(
             for c in range(C):
                 for kind in (Q, K):
                     src = rows[b, c, kind]
-                    on_scalar = b >= B - DRAINING or (c == 1 and kind == Q)
+                    nth_bank = (b * C + c) * 2 + kind
+                    on_scalar = b >= B - DRAINING or nth_bank % SCALAR_EVERY == 0
                     transpose_words(
                         lambda s, u: src[:, s, :].bitcast(F32)[:, u * P : (u + 1) * P],
                         qk_grouped[b][:, c, kind, :],

@@ -18,27 +18,20 @@ PAIRS = 2
 BANK = 512
 PSUM_BANKS = 8
 Q, K = 0, 1
-ROW_TILES = (S + F) // P
 
 STEP_PROJECT = 1
-STEP_TURN = 3
-STEP_SCORE = 4
-
-SCALAR_EVERY = 8
-FILLING = 2
-DRAINING = 1
+STEP_SCORE = 2
 
 FLOPS = 2 * B * S * H * H * C * 2 + 2 * B * C * (S + F) * S * H
 
 
-def load_packed_weight(nc, codes, planes, words, scales):
+def load_planes(nc, planes, scales):
     for quadrant in range(4):
         rows = slice(4 * quadrant, 4 * quadrant + 4)
         nc.sync.dma_start(
             out=planes[32 * quadrant : 32 * quadrant + 4].bitcast(I32),
             in_=scales[:, rows, :].rearrange("g r n -> r g n").bitcast(I32),
         )
-    nc.sync.dma_start(out=codes.bitcast(I32), in_=words.rearrange("g p n t -> p g (n t)").bitcast(I32))
 
 
 def tile_relationtagger_pa_t_e_kernel(
@@ -50,13 +43,14 @@ def tile_relationtagger_pa_t_e_kernel(
         keep = ctx.enter_context(tc.tile_pool(name="keep", bufs=1))
         h_stage = ctx.enter_context(tc.tile_pool(name="h_stage", bufs=2))
         h_quant = ctx.enter_context(tc.tile_pool(name="h_quant", bufs=3))
-        rows_pool = ctx.enter_context(tc.tile_pool(name="rows", bufs=2 * C * (STEP_TURN - STEP_PROJECT + 1)))
-        qk_stage = ctx.enter_context(tc.tile_pool(name="qk_stage", bufs=2))
-        qk_quant = ctx.enter_context(tc.tile_pool(name="qk_quant", bufs=3))
-        out_pool = ctx.enter_context(tc.tile_pool(name="out", bufs=3))
+        qk_stage = ctx.enter_context(tc.tile_pool(name="qk_stage", bufs=4))
+        qk_quant = ctx.enter_context(tc.tile_pool(name="qk_quant", bufs=6))
+        out_pool = ctx.enter_context(tc.tile_pool(name="out", bufs=9))
         psum = ctx.enter_context(tc.psum_pool(name="psum", bufs=PSUM_BANKS))
 
         hid = keep.tile([P, B, TOKEN_TILES, H], BF16, name="hid")
+        w_given = keep.tile([P, 2, C, H], U32, name="w_given", align_bytes=64)
+        w_given_planes = keep.tile([P, 2, C, H], U8, name="w_given_planes", align_bytes=64)
         w_codes = keep.tile([P, 2, C, H], U32, name="w_codes", align_bytes=64)
         w_planes = keep.tile([P, 2, C, H], U8, name="w_planes", align_bytes=64)
         emb_codes = keep.tile([P, C, F], U32, name="emb_codes", align_bytes=64)
@@ -64,47 +58,62 @@ def tile_relationtagger_pa_t_e_kernel(
         gate = keep.tile([P, C, B, S], BF16, name="gate")
         ident = keep.tile([P, P], F32, name="ident")
 
-        nc.vector.memset(w_planes[:].bitcast(I32), 0)
+        nc.vector.memset(w_given_planes[:].bitcast(I32), 0)
         nc.vector.memset(emb_planes[:].bitcast(I32), 0)
         make_identity(nc, ident[:])
 
         def load_hidden(b):
             nc.sync.dma_start(out=hid[:, b], in_=hidden[b].rearrange("(s p) h -> p s h", p=P))
 
+        def load_codes(kind, c, words):
+            nc.sync.dma_start(
+                out=w_given[:, kind, c, :].bitcast(I32), in_=words[c].rearrange("p n t -> p (n t)").bitcast(I32)
+            )
+
         load_hidden(0)
+        load_planes(nc, w_given_planes[:, Q], Wq_scales)
+        load_planes(nc, w_given_planes[:, K], Wk_scales)
+        load_codes(Q, 0, Wq_words)
+        load_codes(K, 0, Wk_words)
         load_hidden(1)
-        load_packed_weight(nc, w_codes[:, Q], w_planes[:, Q], Wq_words, Wq_scales)
-        load_packed_weight(nc, w_codes[:, K], w_planes[:, K], Wk_words, Wk_scales)
-        for b in range(2, STEP_SCORE):
-            load_hidden(b)
-        load_packed_weight(nc, emb_codes[:], emb_planes[:], emb_words, emb_scales)
+        load_codes(Q, 1, Wq_words)
+        load_codes(K, 1, Wk_words)
+        load_hidden(2)
+        load_hidden(3)
+        load_planes(nc, emb_planes[:], emb_scales)
+        nc.sync.dma_start(out=emb_codes[:].bitcast(I32), in_=emb_words.rearrange("g p n t -> p g (n t)").bitcast(I32))
         nc.sync.dma_start(
             out=gate[:].rearrange("p c b j -> p (c b j)"),
             in_=vsum.rearrange("c b j -> (c b j)").partition_broadcast(P),
         )
-        for b in range(STEP_SCORE, B):
+        for b in range(4, B):
             load_hidden(b)
 
-        def transpose_words(word_rows, grouped, copy):
+        def regroup_weight(kind, c):
+            nc.vector.tensor_copy(
+                out=w_codes[:, kind, c, :].bitcast(I32).rearrange("p (t m) -> p t m", t=PACK),
+                in_=w_given[:, kind, c, :].bitcast(I32).rearrange("p (m t) -> p t m", t=PACK),
+            )
+            nc.vector.tensor_copy(
+                out=w_planes[:, kind, c, :].rearrange("p (t m) -> p t m", t=PACK),
+                in_=w_given_planes[:, kind, c, :].rearrange("p (m t) -> p t m", t=PACK),
+            )
+
+        h_grouped, h_codes, h_planes = {}, {}, {}
+        qk_grouped, qk_codes, qk_planes = {}, {}, {}
+
+        def transpose_hidden(b, copy):
+            h_grouped[b] = h_stage.tile([P, PACK * S], BF16, name="h_grouped", align_bytes=64)
             bank = psum.tile([P, BANK], F32, name="bank", tag="bank")
             for s in range(TOKEN_TILES):
                 for u in range(PAIRS):
                     col = (s * PAIRS + u) * P
-                    nc.tensor.transpose(bank[:, col : col + P], word_rows(s, u), ident[:])
+                    nc.tensor.transpose(
+                        bank[:, col : col + P], hid[:, b, s, :].bitcast(F32)[:, u : H // 2 : PAIRS], ident[:]
+                    )
             copy(
-                out=grouped.bitcast(F32).rearrange("p (s j u) -> p s j u", s=TOKEN_TILES, u=PAIRS),
+                out=h_grouped[b][:].bitcast(F32).rearrange("p (s j u) -> p s j u", s=TOKEN_TILES, u=PAIRS),
                 in_=bank[:].rearrange("p (s u j) -> p s j u", s=TOKEN_TILES, u=PAIRS),
-            )
-
-        h_grouped, h_codes, h_planes = {}, {}, {}
-        rows, qk_grouped, qk_codes, qk_planes = {}, {}, {}, {}
-
-        def transpose_hidden(b):
-            h_grouped[b] = h_stage.tile([P, PACK * S], BF16, name="h_grouped", align_bytes=64)
-            transpose_words(
-                lambda s, u: hid[:, b, s, :].bitcast(F32)[:, u : H // 2 : PAIRS],
-                h_grouped[b][:],
-                nc.scalar.copy,
             )
 
         def quantise_hidden(b):
@@ -112,101 +121,97 @@ def tile_relationtagger_pa_t_e_kernel(
             h_planes[b] = h_quant.tile([P, S], U8, name="h_planes", align_bytes=64)
             nc.vector.quantize_mx(out=h_codes[b][:].bitcast(FP8X4), scales=h_planes[b][:], in_=h_grouped[b][:])
 
-        def project(b, c):
+        def project(b, c, copies):
+            qk_grouped[b, c] = qk_stage.tile([P, 2, PACK * S], BF16, name="qk_grouped", align_bytes=64)
             for kind in (Q, K):
-                rows[b, c, kind] = rows_pool.tile([P, TOKEN_TILES, H], BF16, name="rows")
                 for s in range(TOKEN_TILES):
                     tokens = slice(s * P, (s + 1) * P)
                     bank = psum.tile([P, BANK], F32, name="bank", tag="bank")
-                    nc.tensor.matmul_mx(
-                        out=bank[:],
-                        lhsT=h_codes[b][:, tokens].bitcast(FP8X4),
-                        lhsT_scale=h_planes[b][:, tokens],
-                        rhs=w_codes[:, kind, c, :].bitcast(FP8X4),
-                        rhs_scale=w_planes[:, kind, c, :],
-                        start=True,
-                        stop=True,
-                    )
-                    copy = nc.vector.tensor_copy if b < FILLING and s == 1 else nc.scalar.copy
-                    copy(
-                        out=rows[b, c, kind][:, s, :].rearrange("t (u p e) -> t u p e", u=PAIRS, e=2),
-                        in_=bank[:].rearrange("t (p u e) -> t u p e", u=PAIRS, e=2),
-                    )
-
-        def transpose_projections(b):
-            qk_grouped[b] = qk_stage.tile([P, C, 2, PACK * S], BF16, name="qk_grouped", align_bytes=64)
-            for c in range(C):
-                for kind in (Q, K):
-                    src = rows[b, c, kind]
-                    nth_bank = (b * C + c) * 2 + kind
-                    on_scalar = b >= B - DRAINING or nth_bank % SCALAR_EVERY == 0
-                    transpose_words(
-                        lambda s, u: src[:, s, :].bitcast(F32)[:, u * P : (u + 1) * P],
-                        qk_grouped[b][:, c, kind, :],
-                        nc.scalar.copy if on_scalar else nc.vector.tensor_copy,
+                    for t in range(PACK):
+                        features = slice(t * P, (t + 1) * P)
+                        nc.tensor.matmul_mx(
+                            out=bank[:, features],
+                            lhsT=w_codes[:, kind, c, features].bitcast(FP8X4),
+                            lhsT_scale=w_planes[:, kind, c, features],
+                            rhs=h_codes[b][:, tokens].bitcast(FP8X4),
+                            rhs_scale=h_planes[b][:, tokens],
+                            start=True,
+                            stop=True,
+                        )
+                    copies[kind * TOKEN_TILES + s](
+                        out=qk_grouped[b, c][:, kind, s * BANK : (s + 1) * BANK].rearrange("p (j t) -> p j t", t=PACK),
+                        in_=bank[:].rearrange("p (t j) -> p j t", t=PACK),
                     )
 
-        def quantise_projections(b):
-            qk_codes[b] = qk_quant.tile([P, C, 2, S], U32, name="qk_codes", align_bytes=64)
-            qk_planes[b] = qk_quant.tile([P, C, 2, S], U8, name="qk_planes", align_bytes=64)
-            for c in range(C):
-                nc.vector.quantize_mx(
-                    out=qk_codes[b][:, c].rearrange("p k j -> p (k j)").bitcast(FP8X4),
-                    scales=qk_planes[b][:, c].rearrange("p k j -> p (k j)"),
-                    in_=qk_grouped[b][:, c].rearrange("p k x -> p (k x)"),
-                )
+        def quantise_projections(b, c):
+            qk_codes[b, c] = qk_quant.tile([P, 2, S], U32, name="qk_codes", align_bytes=64)
+            qk_planes[b, c] = qk_quant.tile([P, 2, S], U8, name="qk_planes", align_bytes=64)
+            nc.vector.quantize_mx(
+                out=qk_codes[b, c][:].rearrange("p k j -> p (k j)").bitcast(FP8X4),
+                scales=qk_planes[b, c][:].rearrange("p k j -> p (k j)"),
+                in_=qk_grouped[b, c][:].rearrange("p k x -> p (k x)"),
+            )
 
         def score_pass(dst, b, c, lhsT, lhsT_scale):
             nc.tensor.matmul_mx(
                 out=dst,
                 lhsT=lhsT.bitcast(FP8X4),
                 lhsT_scale=lhsT_scale,
-                rhs=qk_codes[b][:, c, K, :].bitcast(FP8X4),
-                rhs_scale=qk_planes[b][:, c, K, :],
+                rhs=qk_codes[b, c][:, K, :].bitcast(FP8X4),
+                rhs_scale=qk_planes[b, c][:, K, :],
                 start=True,
                 stop=True,
             )
 
-        def score(b):
-            result = out_pool.tile([P, C, ROW_TILES, S], F32, name="result")
-            for c in range(C):
-                bank = psum.tile([P, BANK], F32, name="bank", tag="bank")
-                for s in range(TOKEN_TILES):
-                    tokens = slice(s * P, (s + 1) * P)
-                    score_pass(
-                        bank[:, s * S : (s + 1) * S], b, c, qk_codes[b][:, c, Q, tokens], qk_planes[b][:, c, Q, tokens]
-                    )
-                nc.vector.tensor_tensor(
-                    out=result[:, c, 0:TOKEN_TILES, :],
-                    in0=bank[:].rearrange("p (s j) -> p s j", s=TOKEN_TILES),
-                    in1=gate[:, c, b, :].unsqueeze(1).to_broadcast([P, TOKEN_TILES, S]),
-                    op=mybir.AluOpType.mult,
-                )
-                nc.sync.dma_start(
-                    out=out[b, c, 0:S, :].rearrange("(s p) j -> p s j", p=P), in_=result[:, c, 0:TOKEN_TILES, :]
-                )
+        def score_tokens(b, c):
+            result = out_pool.tile([P, TOKEN_TILES, S], F32, name="result")
+            bank = psum.tile([P, BANK], F32, name="bank", tag="bank")
+            for s in range(TOKEN_TILES):
+                tokens = slice(s * P, (s + 1) * P)
+                score_pass(bank[:, s * S : (s + 1) * S], b, c, qk_codes[b, c][:, Q, tokens], qk_planes[b, c][:, Q, tokens])
+            nc.vector.tensor_tensor(
+                out=result[:],
+                in0=bank[:].rearrange("p (s j) -> p s j", s=TOKEN_TILES),
+                in1=gate[:, c, b, :].unsqueeze(1).to_broadcast([P, TOKEN_TILES, S]),
+                op=mybir.AluOpType.mult,
+            )
+            nc.sync.dma_start(out=out[b, c, 0:S, :].rearrange("(s p) j -> p s j", p=P), in_=result[:])
+
+        def score_labels(b):
+            result = out_pool.tile([P, C, S], F32, name="result")
             bank = psum.tile([P, BANK], F32, name="bank", tag="bank")
             for c in range(C):
                 score_pass(bank[:, c * S : (c + 1) * S], b, c, emb_codes[:, c, :], emb_planes[:, c, :])
             nc.vector.tensor_tensor(
-                out=result[:, :, TOKEN_TILES, :],
+                out=result[:],
                 in0=bank[:].rearrange("p (c j) -> p c j", c=C),
                 in1=gate[:, :, b, :],
                 op=mybir.AluOpType.mult,
             )
-            nc.sync.dma_start(out=out[b, :, S:, :].rearrange("c p j -> p c j"), in_=result[:, :, TOKEN_TILES, :])
+            nc.sync.dma_start(out=out[b, :, S:, :].rearrange("c p j -> p c j"), in_=result[:])
 
+        act, dve = nc.scalar.copy, nc.vector.tensor_copy
         for step in range(B + STEP_SCORE):
+            projecting, scoring = step - STEP_PROJECT, step - STEP_SCORE
             if step < B:
-                transpose_hidden(step)
-            if 0 <= step - STEP_TURN < B:
-                transpose_projections(step - STEP_TURN)
-                quantise_projections(step - STEP_TURN)
+                transpose_hidden(step, act if step < 2 else dve)
+            if scoring >= 0:
+                quantise_projections(scoring, 1)
+            if step == 1:
+                regroup_weight(Q, 0)
+                regroup_weight(K, 0)
+            if 0 <= projecting < B:
+                project(projecting, 0, [act, act, act, act])
+            if scoring >= 0:
+                score_tokens(scoring, 0)
             if step < B:
                 quantise_hidden(step)
-            if 0 <= step - STEP_PROJECT < B:
-                project(step - STEP_PROJECT, 0)
-            if 0 <= step - STEP_SCORE < B:
-                score(step - STEP_SCORE)
-            if 0 <= step - STEP_PROJECT < B:
-                project(step - STEP_PROJECT, 1)
+            if step == 1:
+                regroup_weight(Q, 1)
+                regroup_weight(K, 1)
+            if 0 <= projecting < B:
+                quantise_projections(projecting, 0)
+                project(projecting, 1, [dve if projecting % 3 != 0 else act, act, act, act])
+            if scoring >= 0:
+                score_tokens(scoring, 1)
+                score_labels(scoring)

@@ -22,6 +22,13 @@ Q, K = 0, 1
 STEP_PROJECT = 1
 STEP_SCORE = 2
 
+GATE_HEAD = 4
+
+
+def COPIES1(b, act, dve):
+    return [dve, act, dve, act] if b == 0 else [dve if b % 3 != 0 else act, act, act, act]
+
+
 FLOPS = 2 * B * S * H * H * C * 2 + 2 * B * C * (S + F) * S * H
 
 
@@ -55,7 +62,8 @@ def tile_relationtagger_pa_t_e_kernel(
         w_planes = keep.tile([P, 2, C, H], U8, name="w_planes", align_bytes=64)
         emb_codes = keep.tile([P, C, F], U32, name="emb_codes", align_bytes=64)
         emb_planes = keep.tile([P, C, F], U8, name="emb_planes", align_bytes=64)
-        gate = keep.tile([P, C, B, S], BF16, name="gate")
+        gate_head = keep.tile([P, C, GATE_HEAD, S], BF16, name="gate_head")
+        gate_rest = keep.tile([P, C, B - GATE_HEAD, S], BF16, name="gate_rest")
         ident = keep.tile([P, P], F32, name="ident")
 
         nc.vector.memset(w_given_planes[:].bitcast(I32), 0)
@@ -70,33 +78,40 @@ def tile_relationtagger_pa_t_e_kernel(
                 out=w_given[:, kind, c, :].bitcast(I32), in_=words[c].rearrange("p n t -> p (n t)").bitcast(I32)
             )
 
+        def load_gate(tile, first, end):
+            nc.sync.dma_start(
+                out=tile[:].rearrange("p c b j -> p c (b j)"),
+                in_=vsum[:, first:end, :].rearrange("c b j -> c (b j)").partition_broadcast(P),
+            )
+
+        def gate_of(b):
+            return gate_head[:, :, b, :] if b < GATE_HEAD else gate_rest[:, :, b - GATE_HEAD, :]
+
         load_hidden(0)
         load_planes(nc, w_given_planes[:, Q], Wq_scales)
-        load_planes(nc, w_given_planes[:, K], Wk_scales)
         load_codes(Q, 0, Wq_words)
+        load_planes(nc, w_given_planes[:, K], Wk_scales)
         load_codes(K, 0, Wk_words)
         load_hidden(1)
         load_codes(Q, 1, Wq_words)
         load_codes(K, 1, Wk_words)
         load_hidden(2)
+        load_gate(gate_head, 0, GATE_HEAD)
         load_hidden(3)
         load_planes(nc, emb_planes[:], emb_scales)
         nc.sync.dma_start(out=emb_codes[:].bitcast(I32), in_=emb_words.rearrange("g p n t -> p g (n t)").bitcast(I32))
-        nc.sync.dma_start(
-            out=gate[:].rearrange("p c b j -> p (c b j)"),
-            in_=vsum.rearrange("c b j -> (c b j)").partition_broadcast(P),
-        )
+        load_gate(gate_rest, GATE_HEAD, B)
         for b in range(4, B):
             load_hidden(b)
 
         def regroup_weight(kind, c):
             nc.vector.tensor_copy(
-                out=w_codes[:, kind, c, :].bitcast(I32).rearrange("p (t m) -> p t m", t=PACK),
-                in_=w_given[:, kind, c, :].bitcast(I32).rearrange("p (m t) -> p t m", t=PACK),
-            )
-            nc.vector.tensor_copy(
                 out=w_planes[:, kind, c, :].rearrange("p (t m) -> p t m", t=PACK),
                 in_=w_given_planes[:, kind, c, :].rearrange("p (m t) -> p t m", t=PACK),
+            )
+            nc.vector.tensor_copy(
+                out=w_codes[:, kind, c, :].bitcast(I32).rearrange("p (t m) -> p t m", t=PACK),
+                in_=w_given[:, kind, c, :].bitcast(I32).rearrange("p (m t) -> p t m", t=PACK),
             )
 
         h_grouped, h_codes, h_planes = {}, {}, {}
@@ -121,9 +136,9 @@ def tile_relationtagger_pa_t_e_kernel(
             h_planes[b] = h_quant.tile([P, S], U8, name="h_planes", align_bytes=64)
             nc.vector.quantize_mx(out=h_codes[b][:].bitcast(FP8X4), scales=h_planes[b][:], in_=h_grouped[b][:])
 
-        def project(b, c, copies):
+        def project(b, c, copies, kinds=(Q, K)):
             qk_grouped[b, c] = qk_stage.tile([P, 2, PACK * S], BF16, name="qk_grouped", align_bytes=64)
-            for kind in (Q, K):
+            for kind in kinds:
                 for s in range(TOKEN_TILES):
                     tokens = slice(s * P, (s + 1) * P)
                     bank = psum.tile([P, BANK], F32, name="bank", tag="bank")
@@ -142,6 +157,14 @@ def tile_relationtagger_pa_t_e_kernel(
                         out=qk_grouped[b, c][:, kind, s * BANK : (s + 1) * BANK].rearrange("p (j t) -> p j t", t=PACK),
                         in_=bank[:].rearrange("p (t j) -> p j t", t=PACK),
                     )
+
+        def quantise_one(b, c, kind):
+            if (b, c) not in qk_codes:
+                qk_codes[b, c] = qk_quant.tile([P, 2, S], U32, name="qk_codes", align_bytes=64)
+                qk_planes[b, c] = qk_quant.tile([P, 2, S], U8, name="qk_planes", align_bytes=64)
+            nc.vector.quantize_mx(
+                out=qk_codes[b, c][:, kind, :].bitcast(FP8X4), scales=qk_planes[b, c][:, kind, :], in_=qk_grouped[b, c][:, kind, :]
+            )
 
         def quantise_projections(b, c):
             qk_codes[b, c] = qk_quant.tile([P, 2, S], U32, name="qk_codes", align_bytes=64)
@@ -172,7 +195,7 @@ def tile_relationtagger_pa_t_e_kernel(
             nc.vector.tensor_tensor(
                 out=result[:],
                 in0=bank[:].rearrange("p (s j) -> p s j", s=TOKEN_TILES),
-                in1=gate[:, c, b, :].unsqueeze(1).to_broadcast([P, TOKEN_TILES, S]),
+                in1=gate_of(b)[:, c, :].unsqueeze(1).to_broadcast([P, TOKEN_TILES, S]),
                 op=mybir.AluOpType.mult,
             )
             nc.sync.dma_start(out=out[b, c, 0:S, :].rearrange("(s p) j -> p s j", p=P), in_=result[:])
@@ -185,7 +208,7 @@ def tile_relationtagger_pa_t_e_kernel(
             nc.vector.tensor_tensor(
                 out=result[:],
                 in0=bank[:].rearrange("p (c j) -> p c j", c=C),
-                in1=gate[:, :, b, :],
+                in1=gate_of(b),
                 op=mybir.AluOpType.mult,
             )
             nc.sync.dma_start(out=out[b, :, S:, :].rearrange("c p j -> p c j"), in_=result[:])
@@ -193,25 +216,37 @@ def tile_relationtagger_pa_t_e_kernel(
         act, dve = nc.scalar.copy, nc.vector.tensor_copy
         for step in range(B + STEP_SCORE):
             projecting, scoring = step - STEP_PROJECT, step - STEP_SCORE
-            if step < B:
+            last = step == B + STEP_SCORE - 1
+            if step < B and step != 1:
                 transpose_hidden(step, act if step < 2 else dve)
+            if step == 0:
+                regroup_weight(Q, 0)
+            if last:
+                quantise_one(scoring, 1, Q)
+                score_tokens(scoring, 0)
+                score_labels(scoring)
+                score_tokens(scoring, 1)
+                continue
             if scoring >= 0:
                 quantise_projections(scoring, 1)
-            if step == 1:
-                regroup_weight(Q, 0)
-                regroup_weight(K, 0)
             if 0 <= projecting < B:
                 project(projecting, 0, [act, act, act, act])
+            if step == 1:
+                transpose_hidden(step, act)
             if scoring >= 0:
                 score_tokens(scoring, 0)
-            if step < B:
-                quantise_hidden(step)
             if step == 1:
                 regroup_weight(Q, 1)
                 regroup_weight(K, 1)
+            if step < B:
+                quantise_hidden(step)
+            if step == 0:
+                regroup_weight(K, 0)
             if 0 <= projecting < B:
                 quantise_projections(projecting, 0)
-                project(projecting, 1, [dve if projecting % 3 != 0 else act, act, act, act])
+                project(projecting, 1, COPIES1(projecting, act, dve), (K, Q) if projecting == B - 1 else (Q, K))
+            if projecting == B - 1:
+                quantise_one(projecting, 1, K)
             if scoring >= 0:
                 score_tokens(scoring, 1)
                 score_labels(scoring)

@@ -71,7 +71,7 @@ def tile_relationtagger_pa_t_e_kernel(
         make_identity(nc, ident[:])
 
         def load_hidden(b):
-            nc.sync.dma_start(out=hid[:, b], in_=hidden[b].rearrange("(s p) h -> p s h", p=P))
+            nc.sync.dma_start(out=hid[:, b], in_=hidden[b].rearrange("(p s) h -> p s h", s=TOKEN_TILES))
 
         def load_codes(kind, c, words):
             nc.sync.dma_start(
@@ -193,12 +193,15 @@ def tile_relationtagger_pa_t_e_kernel(
                 tokens = slice(s * P, (s + 1) * P)
                 score_pass(bank[:, s * S : (s + 1) * S], b, c, qk_codes[b, c][:, Q, tokens], qk_planes[b, c][:, Q, tokens])
             nc.vector.tensor_tensor(
-                out=result[:],
-                in0=bank[:].rearrange("p (s j) -> p s j", s=TOKEN_TILES),
-                in1=gate_of(b)[:, c, :].unsqueeze(1).to_broadcast([P, TOKEN_TILES, S]),
+                out=result[:].rearrange("p s (m r) -> p s m r", r=TOKEN_TILES),
+                in0=bank[:].rearrange("p (s r m) -> p s m r", s=TOKEN_TILES, r=TOKEN_TILES),
+                in1=gate_of(b)[:, c, :]
+                .rearrange("p (m r) -> p m r", r=TOKEN_TILES)
+                .unsqueeze(1)
+                .to_broadcast([P, TOKEN_TILES, P, TOKEN_TILES]),
                 op=mybir.AluOpType.mult,
             )
-            nc.sync.dma_start(out=out[b, c, 0:S, :].rearrange("(s p) j -> p s j", p=P), in_=result[:])
+            nc.sync.dma_start(out=out[b, c, 0:S, :].rearrange("(p s) j -> p s j", s=TOKEN_TILES), in_=result[:])
 
         def score_labels(b):
             result = out_pool.tile([P, C, S], F32, name="result")
@@ -206,9 +209,9 @@ def tile_relationtagger_pa_t_e_kernel(
             for c in range(C):
                 score_pass(bank[:, c * S : (c + 1) * S], b, c, emb_codes[:, c, :], emb_planes[:, c, :])
             nc.vector.tensor_tensor(
-                out=result[:],
-                in0=bank[:].rearrange("p (c j) -> p c j", c=C),
-                in1=gate_of(b),
+                out=result[:].rearrange("p c (m r) -> p c m r", r=TOKEN_TILES),
+                in0=bank[:].rearrange("p (c r m) -> p c m r", c=C, r=TOKEN_TILES),
+                in1=gate_of(b).rearrange("p c (m r) -> p c m r", r=TOKEN_TILES),
                 op=mybir.AluOpType.mult,
             )
             nc.sync.dma_start(out=out[b, :, S:, :].rearrange("c p j -> p c j"), in_=result[:])

@@ -23,6 +23,7 @@ STEP_PROJECT = 1
 STEP_SCORE = 2
 
 GATE_HEAD = 4
+WARM_BEFORE, WARM_AFTER = 4, 3
 
 
 def COPIES1(b, act, dve):
@@ -69,6 +70,13 @@ def tile_relationtagger_pa_t_e_kernel(
         nc.vector.memset(w_given_planes[:].bitcast(I32), 0)
         nc.vector.memset(emb_planes[:].bitcast(I32), 0)
         make_identity(nc, ident[:])
+        warm = keep.tile([P, BANK], BF16, name="warm")
+        nc.vector.memset(warm[:], 0.0)
+
+        def warm_up(n):
+            bank = psum.tile([P, BANK], F32, name="bank", tag="bank")
+            for i in range(n):
+                nc.tensor.matmul(out=bank[:], lhsT=warm[:, 0:P], rhs=warm[:], start=True, stop=True)
 
         def load_hidden(b):
             nc.sync.dma_start(out=hid[:, b], in_=hidden[b].rearrange("(p s) h -> p s h", s=TOKEN_TILES))
@@ -220,8 +228,12 @@ def tile_relationtagger_pa_t_e_kernel(
         for step in range(B + STEP_SCORE):
             projecting, scoring = step - STEP_PROJECT, step - STEP_SCORE
             last = step == B + STEP_SCORE - 1
+            if step == 0:
+                warm_up(WARM_BEFORE)
             if step < B and step != 1:
                 transpose_hidden(step, act if step < 2 else dve)
+            if step == 0:
+                warm_up(WARM_AFTER)
             if step == 0:
                 regroup_weight(Q, 0)
             if last:

@@ -23,7 +23,7 @@ STEP_PROJECT = 1
 STEP_SCORE = 2
 
 GATE_HEAD = 4
-WARM_BEFORE, WARM_AFTER = 4, 3
+WARM_BEFORE, WARM_AFTER = 4, 6
 
 
 def COPIES1(b, act, dve):

@@ -225,9 +225,8 @@ def tile_relationtagger_pa_t_e_kernel(
             nc.sync.dma_start(out=out[b, :, S:, :].rearrange("c p j -> p c j"), in_=result[:])
 
         act, dve = nc.scalar.copy, nc.vector.tensor_copy
-        for step in range(B + STEP_SCORE):
+        for step in range(B + STEP_SCORE - 1):
             projecting, scoring = step - STEP_PROJECT, step - STEP_SCORE
-            last = step == B + STEP_SCORE - 1
             if step == 0:
                 warm_up(WARM_BEFORE)
             if step < B and step != 1:
@@ -236,12 +235,6 @@ def tile_relationtagger_pa_t_e_kernel(
                 warm_up(WARM_AFTER)
             if step == 0:
                 regroup_weight(Q, 0)
-            if last:
-                quantise_one(scoring, 1, Q)
-                score_tokens(scoring, 0)
-                score_labels(scoring)
-                score_tokens(scoring, 1)
-                continue
             if scoring >= 0:
                 quantise_projections(scoring, 1)
             if 0 <= projecting < B:
@@ -257,11 +250,21 @@ def tile_relationtagger_pa_t_e_kernel(
                 quantise_hidden(step)
             if step == 0:
                 regroup_weight(K, 0)
-            if 0 <= projecting < B:
-                quantise_projections(projecting, 0)
-                project(projecting, 1, COPIES1(projecting, act, dve), (K, Q) if projecting == B - 1 else (Q, K))
             if projecting == B - 1:
+                quantise_projections(projecting, 0)
+                project(projecting, 1, [act, act, act, act], (K,))
+                score_tokens(scoring, 1)
+                score_labels(scoring)
                 quantise_one(projecting, 1, K)
+                project(projecting, 1, [act, act, act, act], (Q,))
+                score_tokens(projecting, 0)
+                quantise_one(projecting, 1, Q)
+                score_labels(projecting)
+                score_tokens(projecting, 1)
+                continue
+            if 0 <= projecting:
+                quantise_projections(projecting, 0)
+                project(projecting, 1, COPIES1(projecting, act, dve))
             if scoring >= 0:
                 score_tokens(scoring, 1)
                 score_labels(scoring)

@@ -67,8 +67,8 @@ def tile_relationtagger_pa_t_e_kernel(
         gate_rest = keep.tile([P, C, B - GATE_HEAD, S], BF16, name="gate_rest")
         ident = keep.tile([P, P], F32, name="ident")
 
-        nc.vector.memset(w_given_planes[:].bitcast(I32), 0)
-        nc.vector.memset(emb_planes[:].bitcast(I32), 0)
+        nc.gpsimd.memset(w_given_planes[:].bitcast(I32), 0)
+        nc.gpsimd.memset(emb_planes[:].bitcast(I32), 0)
         make_identity(nc, ident[:])
         warm = keep.tile([P, BANK], BF16, name="warm")
         nc.vector.memset(warm[:], 0.0)

@@ -22,8 +22,8 @@ Q, K = 0, 1
 STEP_PROJECT = 1
 STEP_SCORE = 2
 
-GATE_HEAD = 4
-WARM_BEFORE, WARM_AFTER = 4, 6
+GATE_RUNS = ((0, 2), (2, 6), (6, B))
+WARM_BEFORE, WARM_AFTER = 4, 4
 
 
 def COPIES1(b, act, dve):
@@ -63,15 +63,27 @@ def tile_relationtagger_pa_t_e_kernel(
         w_planes = keep.tile([P, 2, C, H], U8, name="w_planes", align_bytes=64)
         emb_codes = keep.tile([P, C, F], U32, name="emb_codes", align_bytes=64)
         emb_planes = keep.tile([P, C, F], U8, name="emb_planes", align_bytes=64)
-        gate_head = keep.tile([P, C, GATE_HEAD, S], BF16, name="gate_head")
-        gate_rest = keep.tile([P, C, B - GATE_HEAD, S], BF16, name="gate_rest")
+        gates = []
+        for first, end in GATE_RUNS:
+            tile = keep.tile([P, C, end - first, S], BF16, name="gate%d" % first)
+            gates.append(tile)
         ident = keep.tile([P, P], F32, name="ident")
 
         nc.gpsimd.memset(w_given_planes[:].bitcast(I32), 0)
         nc.gpsimd.memset(emb_planes[:].bitcast(I32), 0)
         make_identity(nc, ident[:])
+        first_gate = keep.tile([P, C, GATE_RUNS[0][1] * S], BF16, name="first_gate")
+        ones = keep.tile([P, P], BF16, name="ones")
         warm = keep.tile([P, BANK], BF16, name="warm")
-        nc.vector.memset(warm[:], 0.0)
+        nc.vector.memset(warm[:].bitcast(I32), 0)
+        nc.vector.memset(first_gate[:].rearrange("p c x -> p (c x)").bitcast(I32), 0)
+        nc.vector.memset(ones[:], 1.0)
+
+        def spread_first_gate(copy):
+            for c in range(C):
+                bank = psum.tile([P, BANK], F32, name="bank", tag="bank")
+                nc.tensor.matmul(out=bank[:], lhsT=ones[:], rhs=first_gate[:, c, :], start=True, stop=True)
+                copy(out=gates[0][:, c].rearrange("p b j -> p (b j)"), in_=bank[:])
 
         def warm_up(n):
             bank = psum.tile([P, BANK], F32, name="bank", tag="bank")
@@ -86,17 +98,22 @@ def tile_relationtagger_pa_t_e_kernel(
                 out=w_given[:, kind, c, :].bitcast(I32), in_=words[c].rearrange("p n t -> p (n t)").bitcast(I32)
             )
 
-        def load_gate(tile, first, end):
+        def load_gate(run):
+            first, end = GATE_RUNS[run]
             nc.sync.dma_start(
-                out=tile[:].rearrange("p c b j -> p c (b j)"),
+                out=gates[run][:].rearrange("p c b j -> p c (b j)"),
                 in_=vsum[:, first:end, :].rearrange("c b j -> c (b j)").partition_broadcast(P),
             )
 
         def gate_of(b):
-            return gate_head[:, :, b, :] if b < GATE_HEAD else gate_rest[:, :, b - GATE_HEAD, :]
+            run = [first <= b < end for first, end in GATE_RUNS].index(True)
+            return gates[run][:, :, b - GATE_RUNS[run][0], :]
 
         load_hidden(0)
         load_planes(nc, w_given_planes[:, Q], Wq_scales)
+        nc.sync.dma_start(
+            out=first_gate[0:1], in_=vsum[:, 0 : GATE_RUNS[0][1], :].rearrange("c b j -> c (b j)").unsqueeze(0)
+        )
         load_codes(Q, 0, Wq_words)
         load_planes(nc, w_given_planes[:, K], Wk_scales)
         load_codes(K, 0, Wk_words)
@@ -104,12 +121,15 @@ def tile_relationtagger_pa_t_e_kernel(
         load_codes(Q, 1, Wq_words)
         load_codes(K, 1, Wk_words)
         load_hidden(2)
-        load_gate(gate_head, 0, GATE_HEAD)
         load_hidden(3)
         load_planes(nc, emb_planes[:], emb_scales)
         nc.sync.dma_start(out=emb_codes[:].bitcast(I32), in_=emb_words.rearrange("g p n t -> p g (n t)").bitcast(I32))
-        load_gate(gate_rest, GATE_HEAD, B)
-        for b in range(4, B):
+        load_hidden(4)
+        load_gate(1)
+        for b in range(5, 8):
+            load_hidden(b)
+        load_gate(2)
+        for b in range(8, B):
             load_hidden(b)
 
         def regroup_weight(kind, c):
@@ -232,6 +252,7 @@ def tile_relationtagger_pa_t_e_kernel(
             if step < B and step != 1:
                 transpose_hidden(step, act if step < 2 else dve)
             if step == 0:
+                spread_first_gate(act)
                 warm_up(WARM_AFTER)
             if step == 0:
                 regroup_weight(Q, 0)

@@ -27,7 +27,7 @@ WARM_BEFORE, WARM_AFTER = 4, 4
 
 
 def COPIES1(b, act, dve):
-    return [dve, act, dve, act] if b == 0 else [dve if b % 3 != 0 else act, act, act, act]
+    return [dve, act, dve, act] if b == 0 else [dve if b % 5 in (1, 3, 4) else act, act, act, act]
 
 
 FLOPS = 2 * B * S * H * H * C * 2 + 2 * B * C * (S + F) * S * H
@@ -115,9 +115,9 @@ def tile_relationtagger_pa_t_e_kernel(
             out=first_gate[0:1], in_=vsum[:, 0 : GATE_RUNS[0][1], :].rearrange("c b j -> c (b j)").unsqueeze(0)
         )
         load_codes(Q, 0, Wq_words)
+        load_hidden(1)
         load_planes(nc, w_given_planes[:, K], Wk_scales)
         load_codes(K, 0, Wk_words)
-        load_hidden(1)
         load_codes(Q, 1, Wq_words)
         load_codes(K, 1, Wk_words)
         load_hidden(2)
@@ -165,7 +165,8 @@ def tile_relationtagger_pa_t_e_kernel(
             nc.vector.quantize_mx(out=h_codes[b][:].bitcast(FP8X4), scales=h_planes[b][:], in_=h_grouped[b][:])
 
         def project(b, c, copies, kinds=(Q, K)):
-            qk_grouped[b, c] = qk_stage.tile([P, 2, PACK * S], BF16, name="qk_grouped", align_bytes=64)
+            if (b, c) not in qk_grouped:
+                qk_grouped[b, c] = qk_stage.tile([P, 2, PACK * S], BF16, name="qk_grouped", align_bytes=64)
             for kind in kinds:
                 for s in range(TOKEN_TILES):
                     tokens = slice(s * P, (s + 1) * P)
@@ -186,12 +187,15 @@ def tile_relationtagger_pa_t_e_kernel(
                         in_=bank[:].rearrange("p (t j) -> p j t", t=PACK),
                     )
 
-        def quantise_one(b, c, kind):
+        def quantise_one(b, c, kind, tiles=range(TOKEN_TILES)):
             if (b, c) not in qk_codes:
                 qk_codes[b, c] = qk_quant.tile([P, 2, S], U32, name="qk_codes", align_bytes=64)
                 qk_planes[b, c] = qk_quant.tile([P, 2, S], U8, name="qk_planes", align_bytes=64)
+            tokens = slice(tiles[0] * P, (tiles[-1] + 1) * P)
             nc.vector.quantize_mx(
-                out=qk_codes[b, c][:, kind, :].bitcast(FP8X4), scales=qk_planes[b, c][:, kind, :], in_=qk_grouped[b, c][:, kind, :]
+                out=qk_codes[b, c][:, kind, tokens].bitcast(FP8X4),
+                scales=qk_planes[b, c][:, kind, tokens],
+                in_=qk_grouped[b, c][:, kind, tiles[0] * BANK : (tiles[-1] + 1) * BANK],
             )
 
         def quantise_projections(b, c):
@@ -231,6 +235,19 @@ def tile_relationtagger_pa_t_e_kernel(
             )
             nc.sync.dma_start(out=out[b, c, 0:S, :].rearrange("(p s) j -> p s j", s=TOKEN_TILES), in_=result[:])
 
+        def score_half(b, c, s):
+            result = out_pool.tile([P, S], F32, name="half")
+            bank = psum.tile([P, BANK], F32, name="bank", tag="bank")
+            tokens = slice(s * P, (s + 1) * P)
+            score_pass(bank[:, 0:S], b, c, qk_codes[b, c][:, Q, tokens], qk_planes[b, c][:, Q, tokens])
+            nc.vector.tensor_tensor(
+                out=result[:].rearrange("p (m r) -> p m r", r=TOKEN_TILES),
+                in0=bank[:, 0:S].rearrange("p (r m) -> p m r", r=TOKEN_TILES),
+                in1=gate_of(b)[:, c, :].rearrange("p (m r) -> p m r", r=TOKEN_TILES),
+                op=mybir.AluOpType.mult,
+            )
+            nc.sync.dma_start(out=out[b, c, 0:S, :].rearrange("(p s) j -> p s j", s=TOKEN_TILES)[:, s, :], in_=result[:])
+
         def score_labels(b):
             result = out_pool.tile([P, C, S], F32, name="result")
             bank = psum.tile([P, BANK], F32, name="bank", tag="bank")
@@ -258,15 +275,16 @@ def tile_relationtagger_pa_t_e_kernel(
                 regroup_weight(Q, 0)
             if scoring >= 0:
                 quantise_projections(scoring, 1)
-            if 0 <= projecting < B:
-                project(projecting, 0, [act, act, act, act])
-            if step == 1:
+            if projecting == 0:
+                project(0, 0, [act, act], (Q,))
+                regroup_weight(Q, 1)
                 transpose_hidden(step, act)
+                project(0, 0, [None, None] + [act, act], (K,))
+                regroup_weight(K, 1)
+            elif 0 <= projecting:
+                project(projecting, 0, [act, act, act, act])
             if scoring >= 0:
                 score_tokens(scoring, 0)
-            if step == 1:
-                regroup_weight(Q, 1)
-                regroup_weight(K, 1)
             if step < B:
                 quantise_hidden(step)
             if step == 0:
@@ -279,13 +297,15 @@ def tile_relationtagger_pa_t_e_kernel(
                 quantise_one(projecting, 1, K)
                 project(projecting, 1, [act, act, act, act], (Q,))
                 score_tokens(projecting, 0)
-                quantise_one(projecting, 1, Q)
+                quantise_one(projecting, 1, Q, (0,))
                 score_labels(projecting)
-                score_tokens(projecting, 1)
+                quantise_one(projecting, 1, Q, (1,))
+                score_half(projecting, 1, 0)
+                score_half(projecting, 1, 1)
                 continue
             if 0 <= projecting:
                 quantise_projections(projecting, 0)
                 project(projecting, 1, COPIES1(projecting, act, dve))
             if scoring >= 0:
-                score_tokens(scoring, 1)
                 score_labels(scoring)
+                score_tokens(scoring, 1)

from contextlib import ExitStack

import concourse.mybir as mybir
from concourse.masks import make_identity

F32 = mybir.dt.float32
BF16 = mybir.dt.bfloat16
U8 = mybir.dt.uint8
U32 = mybir.dt.uint32
I32 = mybir.dt.int32
FP8X4 = mybir.dt.float8_e4m3fn_x4

P = 128
PACK = 4
B, C, S, H, F = 16, 2, 256, 512, 128
TOKEN_TILES = S // P
PAIRS = 2
BANK = 512
PSUM_BANKS = 8
Q, K = 0, 1

STEP_PROJECT = 1
STEP_SCORE = 2

GATE_RUNS = ((0, 2), (2, 6), (6, B))
WARM_BEFORE, WARM_AFTER = 4, 4


def COPIES1(b, act, dve):
    return [dve, act, dve, act] if b == 0 else [dve if b % 5 in (1, 3, 4) else act, act, act, act]


FLOPS = 2 * B * S * H * H * C * 2 + 2 * B * C * (S + F) * S * H


def load_planes(nc, planes, scales):
    for quadrant in range(4):
        rows = slice(4 * quadrant, 4 * quadrant + 4)
        nc.sync.dma_start(
            out=planes[32 * quadrant : 32 * quadrant + 4].bitcast(I32),
            in_=scales[:, rows, :].rearrange("g r n -> r g n").bitcast(I32),
        )


def tile_relationtagger_pa_t_e_kernel(
    tc, hidden, emb_words, emb_scales, Wk_words, Wk_scales, Wq_words, Wq_scales, vsum, out
):
    nc = tc.nc
    with ExitStack() as ctx:
        ctx.enter_context(tc.manual_schedule())
        keep = ctx.enter_context(tc.tile_pool(name="keep", bufs=1))
        h_stage = ctx.enter_context(tc.tile_pool(name="h_stage", bufs=2))
        h_quant = ctx.enter_context(tc.tile_pool(name="h_quant", bufs=3))
        qk_stage = ctx.enter_context(tc.tile_pool(name="qk_stage", bufs=4))
        qk_quant = ctx.enter_context(tc.tile_pool(name="qk_quant", bufs=6))
        out_pool = ctx.enter_context(tc.tile_pool(name="out", bufs=9))
        psum = ctx.enter_context(tc.psum_pool(name="psum", bufs=PSUM_BANKS))

        hid = keep.tile([P, B, TOKEN_TILES, H], BF16, name="hid")
        w_given = keep.tile([P, 2, C, H], U32, name="w_given", align_bytes=64)
        w_given_planes = keep.tile([P, 2, C, H], U8, name="w_given_planes", align_bytes=64)
        w_codes = keep.tile([P, 2, C, H], U32, name="w_codes", align_bytes=64)
        w_planes = keep.tile([P, 2, C, H], U8, name="w_planes", align_bytes=64)
        emb_codes = keep.tile([P, C, F], U32, name="emb_codes", align_bytes=64)
        emb_planes = keep.tile([P, C, F], U8, name="emb_planes", align_bytes=64)
        gates = []
        for first, end in GATE_RUNS:
            tile = keep.tile([P, C, end - first, S], BF16, name="gate%d" % first)
            gates.append(tile)
        ident = keep.tile([P, P], F32, name="ident")

        nc.gpsimd.memset(w_given_planes[:].bitcast(I32), 0)
        nc.gpsimd.memset(emb_planes[:].bitcast(I32), 0)
        make_identity(nc, ident[:])
        first_gate = keep.tile([P, C, GATE_RUNS[0][1] * S], BF16, name="first_gate")
        ones = keep.tile([P, P], BF16, name="ones")
        warm = keep.tile([P, BANK], BF16, name="warm")
        nc.vector.memset(warm[:].bitcast(I32), 0)
        nc.vector.memset(first_gate[:].rearrange("p c x -> p (c x)").bitcast(I32), 0)
        nc.vector.memset(ones[:], 1.0)

        def spread_first_gate(copy):
            for c in range(C):
                bank = psum.tile([P, BANK], F32, name="bank", tag="bank")
                nc.tensor.matmul(out=bank[:], lhsT=ones[:], rhs=first_gate[:, c, :], start=True, stop=True)
                copy(out=gates[0][:, c].rearrange("p b j -> p (b j)"), in_=bank[:])

        def warm_up(n):
            bank = psum.tile([P, BANK], F32, name="bank", tag="bank")
            for i in range(n):
                nc.tensor.matmul(out=bank[:], lhsT=warm[:, 0:P], rhs=warm[:], start=True, stop=True)

        def load_hidden(b):
            nc.sync.dma_start(out=hid[:, b], in_=hidden[b].rearrange("(p s) h -> p s h", s=TOKEN_TILES))

        def load_codes(kind, c, words):
            nc.sync.dma_start(
                out=w_given[:, kind, c, :].bitcast(I32), in_=words[c].rearrange("p n t -> p (n t)").bitcast(I32)
            )

        def load_gate(run):
            first, end = GATE_RUNS[run]
            nc.sync.dma_start(
                out=gates[run][:].rearrange("p c b j -> p c (b j)"),
                in_=vsum[:, first:end, :].rearrange("c b j -> c (b j)").partition_broadcast(P),
            )

        def gate_of(b):
            run = [first <= b < end for first, end in GATE_RUNS].index(True)
            return gates[run][:, :, b - GATE_RUNS[run][0], :]

        load_hidden(0)
        load_planes(nc, w_given_planes[:, Q], Wq_scales)
        nc.sync.dma_start(
            out=first_gate[0:1], in_=vsum[:, 0 : GATE_RUNS[0][1], :].rearrange("c b j -> c (b j)").unsqueeze(0)
        )
        load_codes(Q, 0, Wq_words)
        load_hidden(1)
        load_planes(nc, w_given_planes[:, K], Wk_scales)
        load_codes(K, 0, Wk_words)
        load_codes(Q, 1, Wq_words)
        load_codes(K, 1, Wk_words)
        load_hidden(2)
        load_hidden(3)
        load_planes(nc, emb_planes[:], emb_scales)
        nc.sync.dma_start(out=emb_codes[:].bitcast(I32), in_=emb_words.rearrange("g p n t -> p g (n t)").bitcast(I32))
        load_hidden(4)
        load_gate(1)
        for b in range(5, 8):
            load_hidden(b)
        load_gate(2)
        for b in range(8, B):
            load_hidden(b)

        def regroup_weight(kind, c):
            nc.vector.tensor_copy(
                out=w_planes[:, kind, c, :].rearrange("p (t m) -> p t m", t=PACK),
                in_=w_given_planes[:, kind, c, :].rearrange("p (m t) -> p t m", t=PACK),
            )
            nc.vector.tensor_copy(
                out=w_codes[:, kind, c, :].bitcast(I32).rearrange("p (t m) -> p t m", t=PACK),
                in_=w_given[:, kind, c, :].bitcast(I32).rearrange("p (m t) -> p t m", t=PACK),
            )

        h_grouped, h_codes, h_planes = {}, {}, {}
        qk_grouped, qk_codes, qk_planes = {}, {}, {}

        def transpose_hidden(b, copy):
            h_grouped[b] = h_stage.tile([P, PACK * S], BF16, name="h_grouped", align_bytes=64)
            bank = psum.tile([P, BANK], F32, name="bank", tag="bank")
            for s in range(TOKEN_TILES):
                for u in range(PAIRS):
                    col = (s * PAIRS + u) * P
                    nc.tensor.transpose(
                        bank[:, col : col + P], hid[:, b, s, :].bitcast(F32)[:, u : H // 2 : PAIRS], ident[:]
                    )
            copy(
                out=h_grouped[b][:].bitcast(F32).rearrange("p (s j u) -> p s j u", s=TOKEN_TILES, u=PAIRS),
                in_=bank[:].rearrange("p (s u j) -> p s j u", s=TOKEN_TILES, u=PAIRS),
            )

        def quantise_hidden(b):
            h_codes[b] = h_quant.tile([P, S], U32, name="h_codes", align_bytes=64)
            h_planes[b] = h_quant.tile([P, S], U8, name="h_planes", align_bytes=64)
            nc.vector.quantize_mx(out=h_codes[b][:].bitcast(FP8X4), scales=h_planes[b][:], in_=h_grouped[b][:])

        def project(b, c, copies, kinds=(Q, K)):
            if (b, c) not in qk_grouped:
                qk_grouped[b, c] = qk_stage.tile([P, 2, PACK * S], BF16, name="qk_grouped", align_bytes=64)
            for kind in kinds:
                for s in range(TOKEN_TILES):
                    tokens = slice(s * P, (s + 1) * P)
                    bank = psum.tile([P, BANK], F32, name="bank", tag="bank")
                    for t in range(PACK):
                        features = slice(t * P, (t + 1) * P)
                        nc.tensor.matmul_mx(
                            out=bank[:, features],
                            lhsT=w_codes[:, kind, c, features].bitcast(FP8X4),
                            lhsT_scale=w_planes[:, kind, c, features],
                            rhs=h_codes[b][:, tokens].bitcast(FP8X4),
                            rhs_scale=h_planes[b][:, tokens],
                            start=True,
                            stop=True,
                        )
                    copies[kind * TOKEN_TILES + s](
                        out=qk_grouped[b, c][:, kind, s * BANK : (s + 1) * BANK].rearrange("p (j t) -> p j t", t=PACK),
                        in_=bank[:].rearrange("p (t j) -> p j t", t=PACK),
                    )

        def quantise_one(b, c, kind, tiles=range(TOKEN_TILES)):
            if (b, c) not in qk_codes:
                qk_codes[b, c] = qk_quant.tile([P, 2, S], U32, name="qk_codes", align_bytes=64)
                qk_planes[b, c] = qk_quant.tile([P, 2, S], U8, name="qk_planes", align_bytes=64)
            tokens = slice(tiles[0] * P, (tiles[-1] + 1) * P)
            nc.vector.quantize_mx(
                out=qk_codes[b, c][:, kind, tokens].bitcast(FP8X4),
                scales=qk_planes[b, c][:, kind, tokens],
                in_=qk_grouped[b, c][:, kind, tiles[0] * BANK : (tiles[-1] + 1) * BANK],
            )

        def quantise_projections(b, c):
            qk_codes[b, c] = qk_quant.tile([P, 2, S], U32, name="qk_codes", align_bytes=64)
            qk_planes[b, c] = qk_quant.tile([P, 2, S], U8, name="qk_planes", align_bytes=64)
            nc.vector.quantize_mx(
                out=qk_codes[b, c][:].rearrange("p k j -> p (k j)").bitcast(FP8X4),
                scales=qk_planes[b, c][:].rearrange("p k j -> p (k j)"),
                in_=qk_grouped[b, c][:].rearrange("p k x -> p (k x)"),
            )

        def score_pass(dst, b, c, lhsT, lhsT_scale):
            nc.tensor.matmul_mx(
                out=dst,
                lhsT=lhsT.bitcast(FP8X4),
                lhsT_scale=lhsT_scale,
                rhs=qk_codes[b, c][:, K, :].bitcast(FP8X4),
                rhs_scale=qk_planes[b, c][:, K, :],
                start=True,
                stop=True,
            )

        def score_tokens(b, c):
            result = out_pool.tile([P, TOKEN_TILES, S], F32, name="result")
            bank = psum.tile([P, BANK], F32, name="bank", tag="bank")
            for s in range(TOKEN_TILES):
                tokens = slice(s * P, (s + 1) * P)
                score_pass(bank[:, s * S : (s + 1) * S], b, c, qk_codes[b, c][:, Q, tokens], qk_planes[b, c][:, Q, tokens])
            nc.vector.tensor_tensor(
                out=result[:].rearrange("p s (m r) -> p s m r", r=TOKEN_TILES),
                in0=bank[:].rearrange("p (s r m) -> p s m r", s=TOKEN_TILES, r=TOKEN_TILES),
                in1=gate_of(b)[:, c, :]
                .rearrange("p (m r) -> p m r", r=TOKEN_TILES)
                .unsqueeze(1)
                .to_broadcast([P, TOKEN_TILES, P, TOKEN_TILES]),
                op=mybir.AluOpType.mult,
            )
            nc.sync.dma_start(out=out[b, c, 0:S, :].rearrange("(p s) j -> p s j", s=TOKEN_TILES), in_=result[:])

        def score_half(b, c, s):
            result = out_pool.tile([P, S], F32, name="half")
            bank = psum.tile([P, BANK], F32, name="bank", tag="bank")
            tokens = slice(s * P, (s + 1) * P)
            score_pass(bank[:, 0:S], b, c, qk_codes[b, c][:, Q, tokens], qk_planes[b, c][:, Q, tokens])
            nc.vector.tensor_tensor(
                out=result[:].rearrange("p (m r) -> p m r", r=TOKEN_TILES),
                in0=bank[:, 0:S].rearrange("p (r m) -> p m r", r=TOKEN_TILES),
                in1=gate_of(b)[:, c, :].rearrange("p (m r) -> p m r", r=TOKEN_TILES),
                op=mybir.AluOpType.mult,
            )
            nc.sync.dma_start(out=out[b, c, 0:S, :].rearrange("(p s) j -> p s j", s=TOKEN_TILES)[:, s, :], in_=result[:])

        def score_labels(b):
            result = out_pool.tile([P, C, S], F32, name="result")
            bank = psum.tile([P, BANK], F32, name="bank", tag="bank")
            for c in range(C):
                score_pass(bank[:, c * S : (c + 1) * S], b, c, emb_codes[:, c, :], emb_planes[:, c, :])
            nc.vector.tensor_tensor(
                out=result[:].rearrange("p c (m r) -> p c m r", r=TOKEN_TILES),
                in0=bank[:].rearrange("p (c r m) -> p c m r", c=C, r=TOKEN_TILES),
                in1=gate_of(b).rearrange("p c (m r) -> p c m r", r=TOKEN_TILES),
                op=mybir.AluOpType.mult,
            )
            nc.sync.dma_start(out=out[b, :, S:, :].rearrange("c p j -> p c j"), in_=result[:])

        act, dve = nc.scalar.copy, nc.vector.tensor_copy
        for step in range(B + STEP_SCORE - 1):
            projecting, scoring = step - STEP_PROJECT, step - STEP_SCORE
            if step == 0:
                warm_up(WARM_BEFORE)
            if step < B and step != 1:
                transpose_hidden(step, act if step < 2 else dve)
            if step == 0:
                spread_first_gate(act)
                warm_up(WARM_AFTER)
            if step == 0:
                regroup_weight(Q, 0)
            if scoring >= 0:
                quantise_projections(scoring, 1)
            if projecting == 0:
                project(0, 0, [act, act], (Q,))
                regroup_weight(Q, 1)
                transpose_hidden(step, act)
                project(0, 0, [None, None] + [act, act], (K,))
                regroup_weight(K, 1)
            elif 0 <= projecting:
                project(projecting, 0, [act, act, act, act])
            if scoring >= 0:
                score_tokens(scoring, 0)
            if step < B:
                quantise_hidden(step)
            if step == 0:
                regroup_weight(K, 0)
            if projecting == B - 1:
                quantise_projections(projecting, 0)
                project(projecting, 1, [act, act, act, act], (K,))
                score_tokens(scoring, 1)
                score_labels(scoring)
                quantise_one(projecting, 1, K)
                project(projecting, 1, [act, act, act, act], (Q,))
                score_tokens(projecting, 0)
                quantise_one(projecting, 1, Q, (0,))
                score_labels(projecting)
                quantise_one(projecting, 1, Q, (1,))
                score_half(projecting, 1, 0)
                score_half(projecting, 1, 1)
                continue
            if 0 <= projecting:
                quantise_projections(projecting, 0)
                project(projecting, 1, COPIES1(projecting, act, dve))
            if scoring >= 0:
                score_labels(scoring)
                score_tokens(scoring, 1)
